import numpy as np
import ml_dtypes


def mxq(x, axis, fmt="e4m3"):
    dtype, down = {"e4m3": (ml_dtypes.float8_e4m3fn, 7), "e5m2": (ml_dtypes.float8_e5m2, 14)}[fmt]
    v = np.moveaxis(np.asarray(x, np.float32).astype(ml_dtypes.bfloat16).astype(np.float64), axis, -1)
    blocks = v.reshape(v.shape[:-1] + (-1, 32))
    amax = np.abs(blocks).max(-1, keepdims=True)
    byte = np.maximum(np.where(amax > 0, np.frexp(amax)[1] - 1 + 127, 0) - down, 1)
    scale = np.exp2(byte - 127.0)
    codes = (blocks / scale).astype(np.float32).astype(dtype).astype(np.float64)
    return np.moveaxis((codes * scale).reshape(v.shape), -1, axis)


WIDE = False


def mx_kscale(k):
    if not WIDE:
        return np.ones(k)
    levels = np.array([10, -10, 5, -5, 0])
    a = np.random.permutation(np.resize(levels, k // 512 * 4)).reshape(k // 512, 4)
    idx = np.arange(k)
    return np.exp2(a[idx // 512, idx % 128 // 32])


BF16 = ml_dtypes.bfloat16


def bf(x):
    return np.asarray(x, np.float32).astype(BF16)


def f64(x):
    return np.asarray(x).astype(np.float64)


B, L, D, S, DV = 4, 2048, 1024, 512, 128


def erf(z):
    z = np.clip(f64(z), -6.0, 6.0)
    a = 2.0 * z * z
    term = 2.0 / np.sqrt(np.pi) * z * np.exp(-z * z)
    total = term.copy()
    for n in range(1, 110):
        term *= a
        term /= 2.0 * n + 1.0
        total += term
    return total


def gelu_erf(v):
    return 0.5 * v * (1.0 + erf(v / np.sqrt(2.0)))


def setup_inputs():
    s = mx_kscale(D)
    return {"inputs": bf(np.random.standard_normal((B, L, D)) * s),
            "key_param_tokens": bf(np.random.standard_normal((S, D)) / np.sqrt(D) / s),
            "value_param_tokens": bf(np.random.standard_normal((S, DV)) / np.sqrt(S))}


def reference(inputs, key_param_tokens, value_param_tokens):
    scores = mxq(f64(inputs), 2, "e4m3") @ mxq(f64(key_param_tokens), 1, "e4m3").T
    g = gelu_erf(scores)
    l2 = np.sqrt((g * g).sum(-1, keepdims=True))
    w = g / l2 * np.sqrt(float(g.shape[-1]))
    return mxq(w, 2, "e4m3") @ mxq(f64(value_param_tokens), 0, "e4m3")

@@ -1,0 +1,294 @@
+from contextlib import ExitStack
+import math
+
+import concourse.bass as bass
+import concourse.mybir as mybir
+import concourse.tile as tile
+from concourse.masks import make_identity
+
+F32 = mybir.dt.float32
+BF16 = mybir.dt.bfloat16
+U32 = mybir.dt.uint32
+U8 = mybir.dt.uint8
+FP8X4 = mybir.dt.float8_e4m3fn_x4
+ACT = mybir.ActivationFunctionType
+ALU = mybir.AluOpType
+
+P = 128
+TOKENS = 8192
+D = 1024
+S = 512
+DV = 128
+N_QUADS = TOKENS // (4 * P)
+N_PAIRS = 2 * N_QUADS
+FLOPS = 2 * TOKENS * D * S + 2 * TOKENS * S * DV
+
+MANUAL = True
+AHEAD = 3
+XBUFS = 5
+F_ON_S = (1, 3)
+F_MOD = 5
+E_ENG = "vector"
+SC_BUFS = 3
+WT_BUFS = 2
+
+
+def tile_pattention_t_kernel(tc, inputs, key_param_tokens, value_param_tokens, out):
+    nc = tc.nc
+    xv = inputs.flatten_outer_dims().rearrange("(n p j) d -> n p (j d)", p=P, j=4)
+    ov = out.flatten_outer_dims().rearrange("(n p j) v -> n p (j v)", p=P, j=4)
+    kv = key_param_tokens.rearrange("(p t) d -> p (t d)", t=4)
+    vv = value_param_tokens.rearrange("(p j) v -> p (j v)", j=4)
+
+    with ExitStack() as ctx:
+        const = ctx.enter_context(tc.tile_pool(name="const", bufs=1))
+        xin = ctx.enter_context(tc.tile_pool(name="xin", bufs=XBUFS))
+        xgp = ctx.enter_context(tc.tile_pool(name="xgp", bufs=3))
+        xqp = ctx.enter_context(tc.tile_pool(name="xqp", bufs=3))
+        gp = ctx.enter_context(tc.tile_pool(name="gp", bufs=8))
+        sp = ctx.enter_context(tc.tile_pool(name="sp", bufs=4))
+        wp = ctx.enter_context(tc.tile_pool(name="wp", bufs=6))
+        wgp = ctx.enter_context(tc.tile_pool(name="wgp", bufs=3))
+        wqp = ctx.enter_context(tc.tile_pool(name="wqp", bufs=3))
+        obp = ctx.enter_context(tc.tile_pool(name="obp", bufs=3))
+        psx = ctx.enter_context(tc.psum_pool(name="psx", bufs=2))
+        pss = ctx.enter_context(tc.psum_pool(name="pss", bufs=SC_BUFS))
+        psw = ctx.enter_context(tc.psum_pool(name="psw", bufs=WT_BUFS))
+        pso = ctx.enter_context(tc.psum_pool(name="pso", bufs=1))
+        if MANUAL:
+            ctx.enter_context(tc.manual_schedule())
+
+        st = {}
+
+        warm = const.tile([P, 1], F32, name="warm")
+        nc.vector.memset(warm[:], 0.0)
+        nc.scalar.activation(out=warm[:], in_=warm[:], func=ACT.Gelu)
+        neg_half = const.tile([P, 2], F32, name="neg_half")
+        nc.vector.memset(neg_half[:], -0.5)
+        idf = const.tile([P, P], F32, name="idf")
+        make_identity(nc, idf[:])
+        idb = const.tile([P, P], BF16, name="idb")
+        make_identity(nc, idb[:])
+
+        k_sb = const.tile([P, 4 * D], BF16, name="k_sb")
+        for t in range(4):
+            nc.sync.dma_start(out=k_sb[:, t * D : (t + 1) * D], in_=kv[:, t * D : (t + 1) * D])
+
+        def load(quad, pieces=1):
+            if quad >= N_QUADS:
+                return
+            x_sb = xin.tile([P, 4 * D], BF16, name="x_sb")
+            step = 4 * D // pieces
+            for c in range(0, 4 * D, step):
+                nc.sync.dma_start(out=x_sb[:, c : c + step], in_=xv[quad, :, c : c + step])
+            st["x", quad] = x_sb
+
+        load(0, pieces=2)
+        v_sb = const.tile([P, 4 * DV], BF16, name="v_sb")
+        nc.sync.dma_start(out=v_sb[:], in_=vv)
+        for quad in range(1, AHEAD):
+            load(quad)
+
+        kg = const.tile([P, 4 * D], BF16, name="kg", align_bytes=64)
+        kgw = kg[:].bitcast(F32).rearrange("p (g t r u) -> p g t r u", g=2, t=4, r=P, u=2)
+        kq = const.tile([P, 2 * S], U32, name="kq", align_bytes=64)
+        ks = const.tile([P, 2 * S], U8, name="ks", align_bytes=64)
+        kw = k_sb[:].bitcast(F32)
+        for t in range(4):
+            kt = psx.tile([P, 2, 2, P], F32, name="xt")
+            for g in range(2):
+                for u in range(2):
+                    c = (4 * t + 2 * g + u) * P
+                    nc.tensor.transpose(out=kt[:, g, u, :], in_=kw[:, c : c + P], identity=idf[:])
+            src = kt[:].rearrange("p g u r -> p g r u")
+            if t % 2 == 0:
+                nc.vector.tensor_copy(out=kgw[:, :, t], in_=src)
+            else:
+                nc.scalar.copy(out=kgw[:, :, t], in_=src)
+        for g in range(2):
+            nc.vector.quantize_mx(
+                out=kq[:, g * S : (g + 1) * S].bitcast(FP8X4),
+                scales=ks[:, g * S : (g + 1) * S],
+                in_=kg[:, g * 4 * S : (g + 1) * 4 * S],
+            )
+
+        vg = const.tile([P, 4 * DV], BF16, name="vg", align_bytes=64)
+        vq = const.tile([P, DV], U32, name="vq", align_bytes=64)
+        vs = const.tile([P, DV], U8, name="vs", align_bytes=64)
+
+        def prep_v():
+            nc.vector.tensor_copy(
+                out=vg[:].rearrange("p (v j) -> p v j", j=4),
+                in_=v_sb[:].rearrange("p (j v) -> p v j", j=4),
+            )
+            nc.vector.quantize_mx(out=vq[:].bitcast(FP8X4), scales=vs[:], in_=vg[:])
+
+        def ok(q):
+            return 0 <= q < N_PAIRS
+
+        def tx(q):
+            if not ok(q):
+                return
+            xw = st["x", q // 2][:].bitcast(F32)
+            for h in range(2):
+                j = 2 * (q % 2) + h
+                xt = psx.tile([P, 2, 2, P], F32, name="xt")
+                for g in range(2):
+                    for u in range(2):
+                        c = (4 * j + 2 * g + u) * P
+                        nc.tensor.transpose(out=xt[:, g, u, :], in_=xw[:, c : c + P], identity=idf[:])
+                st["xt", q, h] = xt
+
+        def a(q):
+            if not ok(q):
+                return
+            xg = xgp.tile([P, 2 * D], BF16, name="xg", align_bytes=64)
+            xgw = xg[:].bitcast(F32).rearrange("p (h g r u) -> p h g r u", h=2, g=2, r=P, u=2)
+            for h in range(2):
+                nc.vector.tensor_copy(out=xgw[:, h], in_=st["xt", q, h][:].rearrange("p g u r -> p g r u"))
+            st["xg", q] = xg
+
+        def b(q):
+            if not ok(q):
+                return
+            xq = xqp.tile([P, D // 2], U32, name="xq", align_bytes=64)
+            xs = xqp.tile([P, D // 2], U8, name="xs", align_bytes=64)
+            nc.vector.quantize_mx(out=xq[:].bitcast(FP8X4), scales=xs[:], in_=st["xg", q][:])
+            st["xq", q] = (xq, xs)
+
+        def m1(q):
+            if not ok(q):
+                return
+            xq, xs = st["xq", q]
+            for h in range(2):
+                sc = pss.tile([P, S], F32, name="sc")
+                for g in range(2):
+                    c = (2 * h + g) * P
+                    nc.tensor.matmul_mx(
+                        out=sc[:],
+                        lhsT=xq[:, c : c + P].bitcast(FP8X4),
+                        lhsT_scale=xs[:, c : c + P],
+                        rhs=kq[:, g * S : (g + 1) * S].bitcast(FP8X4),
+                        rhs_scale=ks[:, g * S : (g + 1) * S],
+                        start=(g == 0),
+                        stop=(g == 1),
+                    )
+                st["sc", q, h] = sc
+
+        def c_(q):
+            if not ok(q):
+                return
+            for h in range(2):
+                gt = gp.tile([P, S], F32, name="gt")
+                nc.scalar.activation(out=gt[:], in_=st["sc", q, h][:], func=ACT.Gelu)
+                st["g", q, h] = gt
+
+        def d_(q):
+            if not ok(q):
+                return
+            ss = sp.tile([P, 2], F32, name="ss")
+            for h in range(2):
+                junk = sp.tile([P, S], BF16, name="junk")
+                nc.scalar.activation(
+                    out=junk[:], in_=st["g", q, h][:], func=ACT.Square,
+                    scale=1.0 / math.sqrt(float(S)), accum_out=ss[:, h : h + 1],
+                )
+            st["ss", q] = ss
+
+        def p_(q):
+            if not ok(q):
+                return
+            r = sp.tile([P, 2], F32, name="r")
+            nc.gpsimd.tensor_tensor(out=r[:], in0=st["ss", q][:], in1=neg_half[:], op=ALU.pow)
+            st["r", q] = r
+
+        def e(q):
+            if not ok(q):
+                return
+            for h in range(2):
+                w = wp.tile([P, S], BF16, name="w")
+                if E_ENG == "vector":
+                    nc.vector.tensor_scalar(out=w[:], in0=st["g", q, h][:], scalar1=st["r", q][:, h : h + 1],
+                                            scalar2=None, op0=ALU.mult)
+                else:
+                    nc.gpsimd.tensor_scalar(out=w[:], in0=st["g", q, h][:], scalar1=st["r", q][:, h : h + 1],
+                                            scalar2=0.0, op0=ALU.mult, op1=ALU.add)
+                st["w", q, h] = w
+
+        def tw(q):
+            if not ok(q):
+                return
+            wt = psw.tile([P, 2, 4, P], BF16, name="wt")
+            for h in range(2):
+                w = st["w", q, h]
+                for t in range(4):
+                    nc.tensor.transpose(out=wt[:, h, t, :], in_=w[:, t * P : (t + 1) * P], identity=idb[:])
+            st["wt", q] = wt
+
+        def f_on_s(q):
+            return q % F_MOD in F_ON_S
+
+        def f(q):
+            if not ok(q):
+                return
+            wg = wgp.tile([P, 2 * S], BF16, name="wg", align_bytes=64)
+            dst = wg[:].rearrange("p (h r t) -> p h r t", h=2, r=P, t=4)
+            src = st["wt", q][:].rearrange("p h t r -> p h r t")
+            if f_on_s(q):
+                nc.scalar.copy(out=dst, in_=src)
+            else:
+                nc.vector.tensor_copy(out=dst, in_=src)
+            st["wg", q] = wg
+
+        def g_(q):
+            if not ok(q):
+                return
+            wq = wqp.tile([P, 2 * P], U32, name="wq", align_bytes=64)
+            ws = wqp.tile([P, 2 * P], U8, name="ws", align_bytes=64)
+            nc.vector.quantize_mx(out=wq[:].bitcast(FP8X4), scales=ws[:], in_=st["wg", q][:])
+            st["wq", q] = (wq, ws)
+
+        def m2(q):
+            if not ok(q):
+                return
+            if q % 2 == 0:
+                ot = pso.tile([P, 4, DV], F32, name="ot")
+                st["ot", q // 2] = ot
+            ot = st["ot", q // 2]
+            wq, ws = st["wq", q]
+            for h in range(2):
+                nc.tensor.matmul_mx(
+                    out=ot[:, 2 * (q % 2) + h, :],
+                    lhsT=wq[:, h * P : (h + 1) * P].bitcast(FP8X4),
+                    lhsT_scale=ws[:, h * P : (h + 1) * P],
+                    rhs=vq[:].bitcast(FP8X4),
+                    rhs_scale=vs[:],
+                    start=True,
+                    stop=True,
+                )
+
+        def h_(q):
+            if not ok(q) or q % 2 == 0:
+                return
+            ob = obp.tile([P, 4 * DV], F32, name="ob")
+            nc.scalar.copy(out=ob[:], in_=st["ot", q // 2][:].rearrange("p j v -> p (j v)"))
+            nc.sync.dma_start(out=ov[q // 2], in_=ob[:])
+
+        for n in range(N_PAIRS + 6):
+            if n % 2 == 0:
+                load(n // 2 + AHEAD)
+            b(n - 1)
+            tx(n)
+            tw(n - 3)
+            a(n)
+            d_(n - 2)
+            p_(n - 2)
+            if n == 1:
+                prep_v()
+            f(n - 3)
+            h_(n - 5)
+            m1(n - 1)
+            m2(n - 4)
+            e(n - 2)
+            g_(n - 3)
+            c_(n - 1)

@@ -26,8 +26,8 @@ FLOPS = 2 * TOKENS * D * S + 2 * TOKENS * S * DV
 MANUAL = True
 AHEAD = 3
 XBUFS = 5
-F_ON_S = (1, 3)
-F_MOD = 5
+F_ON_S = (1,)
+F_MOD = 2
 E_ENG = "vector"
 SC_BUFS = 3
 WT_BUFS = 2
@@ -274,21 +274,21 @@ def tile_pattention_t_kernel(tc, inputs, key_param_tokens, value_param_tokens, o
             nc.scalar.copy(out=ob[:], in_=st["ot", q // 2][:].rearrange("p j v -> p (j v)"))
             nc.sync.dma_start(out=ov[q // 2], in_=ob[:])
 
-        for n in range(N_PAIRS + 6):
+        for n in range(N_PAIRS + 7):
             if n % 2 == 0:
                 load(n // 2 + AHEAD)
             b(n - 1)
             tx(n)
-            tw(n - 3)
+            tw(n - 4)
             a(n)
             d_(n - 2)
             p_(n - 2)
             if n == 1:
                 prep_v()
-            f(n - 3)
-            h_(n - 5)
+            f(n - 4)
+            h_(n - 6)
             m1(n - 1)
-            m2(n - 4)
-            e(n - 2)
-            g_(n - 3)
+            m2(n - 5)
+            e(n - 3)
+            g_(n - 4)
             c_(n - 1)

@@ -37,8 +37,8 @@ def tile_pattention_t_kernel(tc, inputs, key_param_tokens, value_param_tokens, o
     nc = tc.nc
     xv = inputs.flatten_outer_dims().rearrange("(n p j) d -> n p (j d)", p=P, j=4)
     ov = out.flatten_outer_dims().rearrange("(n p j) v -> n p (j v)", p=P, j=4)
-    kv = key_param_tokens.rearrange("(p t) d -> p (t d)", t=4)
-    vv = value_param_tokens.rearrange("(p j) v -> p (j v)", j=4)
+    kv = key_param_tokens.rearrange("(t p) d -> t p d", p=P)
+    vv = value_param_tokens.rearrange("(u p e) v -> p u (e v)", u=2, e=2)
 
     with ExitStack() as ctx:
         const = ctx.enter_context(tc.tile_pool(name="const", bufs=1))
@@ -67,12 +67,10 @@ def tile_pattention_t_kernel(tc, inputs, key_param_tokens, value_param_tokens, o
         nc.vector.memset(neg_half[:], -0.5)
         idf = const.tile([P, P], F32, name="idf")
         make_identity(nc, idf[:])
-        idb = const.tile([P, P], BF16, name="idb")
-        make_identity(nc, idb[:])
 
         k_sb = const.tile([P, 4 * D], BF16, name="k_sb")
         for t in range(4):
-            nc.sync.dma_start(out=k_sb[:, t * D : (t + 1) * D], in_=kv[:, t * D : (t + 1) * D])
+            nc.sync.dma_start(out=k_sb[:, t * D : (t + 1) * D], in_=kv[t])
 
         def load(quad, pieces=1):
             if quad >= N_QUADS:
@@ -85,7 +83,7 @@ def tile_pattention_t_kernel(tc, inputs, key_param_tokens, value_param_tokens, o
 
         load(0, pieces=2)
         v_sb = const.tile([P, 4 * DV], BF16, name="v_sb")
-        nc.sync.dma_start(out=v_sb[:], in_=vv)
+        nc.sync.dma_start(out=v_sb[:].rearrange("p (u c) -> p u c", u=2), in_=vv)
         for quad in range(1, AHEAD):
             load(quad)
 
@@ -218,11 +216,11 @@ def tile_pattention_t_kernel(tc, inputs, key_param_tokens, value_param_tokens, o
         def tw(q):
             if not ok(q):
                 return
-            wt = psw.tile([P, 2, 4, P], BF16, name="wt")
+            wt = psw.tile([P, 2, 2, P], F32, name="wt")
             for h in range(2):
-                w = st["w", q, h]
-                for t in range(4):
-                    nc.tensor.transpose(out=wt[:, h, t, :], in_=w[:, t * P : (t + 1) * P], identity=idb[:])
+                ww = st["w", q, h][:].bitcast(F32)
+                for u in range(2):
+                    nc.tensor.transpose(out=wt[:, h, u, :], in_=ww[:, u * P : (u + 1) * P], identity=idf[:])
             st["wt", q] = wt
 
         def f_on_s(q):
@@ -232,8 +230,8 @@ def tile_pattention_t_kernel(tc, inputs, key_param_tokens, value_param_tokens, o
             if not ok(q):
                 return
             wg = wgp.tile([P, 2 * S], BF16, name="wg", align_bytes=64)
-            dst = wg[:].rearrange("p (h r t) -> p h r t", h=2, r=P, t=4)
-            src = st["wt", q][:].rearrange("p h t r -> p h r t")
+            dst = wg[:].bitcast(F32).rearrange("p (h r u) -> p h r u", h=2, r=P, u=2)
+            src = st["wt", q][:].rearrange("p h u r -> p h r u")
             if f_on_s(q):
                 nc.scalar.copy(out=dst, in_=src)
             else:

@@ -28,6 +28,7 @@ AHEAD = 3
 XBUFS = 5
 F_ON_S = (1,)
 F_MOD = 2
+D_ON_V = 30
 E_ENG = "vector"
 SC_BUFS = 3
 WT_BUFS = 2
@@ -93,7 +94,10 @@ def tile_pattention_t_kernel(tc, inputs, key_param_tokens, value_param_tokens, o
         ks = const.tile([P, 2 * S], U8, name="ks", align_bytes=64)
         kw = k_sb[:].bitcast(F32)
         for t in range(4):
-            kt = psx.tile([P, 2, 2, P], F32, name="xt")
+            if t < 2:
+                kt = psx.tile([P, 2, 2, P], F32, name="xt")
+            else:
+                kt = pss.tile([P, 2, 2, P], F32, name="sc")
             for g in range(2):
                 for u in range(2):
                     c = (4 * t + 2 * g + u) * P
@@ -103,7 +107,8 @@ def tile_pattention_t_kernel(tc, inputs, key_param_tokens, value_param_tokens, o
                 nc.vector.tensor_copy(out=kgw[:, :, t], in_=src)
             else:
                 nc.scalar.copy(out=kgw[:, :, t], in_=src)
-        for g in range(2):
+
+        def kb(g):
             nc.vector.quantize_mx(
                 out=kq[:, g * S : (g + 1) * S].bitcast(FP8X4),
                 scales=ks[:, g * S : (g + 1) * S],
@@ -124,35 +129,49 @@ def tile_pattention_t_kernel(tc, inputs, key_param_tokens, value_param_tokens, o
         def ok(q):
             return 0 <= q < N_PAIRS
 
-        def tx(q):
-            if not ok(q):
-                return
+        def tx1(q, h):
             xw = st["x", q // 2][:].bitcast(F32)
-            for h in range(2):
-                j = 2 * (q % 2) + h
-                xt = psx.tile([P, 2, 2, P], F32, name="xt")
-                for g in range(2):
-                    for u in range(2):
-                        c = (4 * j + 2 * g + u) * P
-                        nc.tensor.transpose(out=xt[:, g, u, :], in_=xw[:, c : c + P], identity=idf[:])
-                st["xt", q, h] = xt
+            j = 2 * (q % 2) + h
+            xt = psx.tile([P, 2, 2, P], F32, name="xt")
+            for g in range(2):
+                for u in range(2):
+                    c = (4 * j + 2 * g + u) * P
+                    nc.tensor.transpose(out=xt[:, g, u, :], in_=xw[:, c : c + P], identity=idf[:])
+            st["xt", q, h] = xt
+
+        def tx(q):
+            if ok(q):
+                tx1(q, 0)
+                tx1(q, 1)
+
+        def a1(q, h, on_scalar=False):
+            if h == 0:
+                xg = xgp.tile([P, 2 * D], BF16, name="xg", align_bytes=64)
+                st["xg", q] = xg
+            xgw = st["xg", q][:].bitcast(F32).rearrange("p (h g r u) -> p h g r u", h=2, g=2, r=P, u=2)
+            src = st["xt", q, h][:].rearrange("p g u r -> p g r u")
+            if on_scalar:
+                nc.scalar.copy(out=xgw[:, h], in_=src)
+            else:
+                nc.vector.tensor_copy(out=xgw[:, h], in_=src)
 
         def a(q):
-            if not ok(q):
-                return
-            xg = xgp.tile([P, 2 * D], BF16, name="xg", align_bytes=64)
-            xgw = xg[:].bitcast(F32).rearrange("p (h g r u) -> p h g r u", h=2, g=2, r=P, u=2)
-            for h in range(2):
-                nc.vector.tensor_copy(out=xgw[:, h], in_=st["xt", q, h][:].rearrange("p g u r -> p g r u"))
-            st["xg", q] = xg
+            if ok(q):
+                a1(q, 0)
+                a1(q, 1)
 
-        def b(q):
+        def b(q, halves=(0, 2)):
             if not ok(q):
                 return
-            xq = xqp.tile([P, D // 2], U32, name="xq", align_bytes=64)
-            xs = xqp.tile([P, D // 2], U8, name="xs", align_bytes=64)
-            nc.vector.quantize_mx(out=xq[:].bitcast(FP8X4), scales=xs[:], in_=st["xg", q][:])
-            st["xq", q] = (xq, xs)
+            h0, h1 = halves
+            if h0 == 0:
+                xq = xqp.tile([P, D // 2], U32, name="xq", align_bytes=64)
+                xs = xqp.tile([P, D // 2], U8, name="xs", align_bytes=64)
+                st["xq", q] = (xq, xs)
+            xq, xs = st["xq", q]
+            cols = slice(h0 * D // 4, h1 * D // 4)
+            nc.vector.quantize_mx(out=xq[:, cols].bitcast(FP8X4), scales=xs[:, cols],
+                                  in_=st["xg", q][:, h0 * D : h1 * D])
 
         def m1(q):
             if not ok(q):
@@ -186,11 +205,19 @@ def tile_pattention_t_kernel(tc, inputs, key_param_tokens, value_param_tokens, o
                 return
             ss = sp.tile([P, 2], F32, name="ss")
             for h in range(2):
-                junk = sp.tile([P, S], BF16, name="junk")
-                nc.scalar.activation(
-                    out=junk[:], in_=st["g", q, h][:], func=ACT.Square,
-                    scale=1.0 / math.sqrt(float(S)), accum_out=ss[:, h : h + 1],
-                )
+                g = st["g", q, h]
+                if h == 1 and q >= D_ON_V:
+                    junk = sp.tile([P, S], BF16, name="junkv")
+                    nc.vector.scalar_tensor_tensor(
+                        out=junk[:], in0=g[:], scalar=1.0 / S, in1=g[:],
+                        op0=ALU.mult, op1=ALU.mult, accum_out=ss[:, h : h + 1],
+                    )
+                else:
+                    junk = sp.tile([P, S], BF16, name="junk")
+                    nc.scalar.activation(
+                        out=junk[:], in_=g[:], func=ACT.Square,
+                        scale=1.0 / math.sqrt(float(S)), accum_out=ss[:, h : h + 1],
+                    )
             st["ss", q] = ss
 
         def p_(q):
@@ -272,21 +299,38 @@ def tile_pattention_t_kernel(tc, inputs, key_param_tokens, value_param_tokens, o
             nc.scalar.copy(out=ob[:], in_=st["ot", q // 2][:].rearrange("p j v -> p (j v)"))
             nc.sync.dma_start(out=ov[q // 2], in_=ob[:])
 
-        for n in range(N_PAIRS + 7):
+        tx1(0, 0)
+        tx1(0, 1)
+        a1(0, 0, True)
+        kb(0)
+        b(0, (0, 1))
+        kb(1)
+        a1(0, 1, True)
+        load(AHEAD)
+        tx1(1, 0)
+        a1(1, 0, True)
+        tx1(1, 1)
+        b(0, (1, 2))
+        a1(1, 1)
+        m1(0)
+        prep_v()
+        c_(0)
+        for n in range(2, N_PAIRS + 8):
             if n % 2 == 0:
                 load(n // 2 + AHEAD)
             b(n - 1)
+            g_(n - 5)
             tx(n)
             tw(n - 4)
             a(n)
             d_(n - 2)
             p_(n - 2)
-            if n == 1:
-                prep_v()
-            f(n - 4)
-            h_(n - 6)
+            if f_on_s(n - 4):
+                f(n - 4)
+            h_(n - 7)
             m1(n - 1)
-            m2(n - 5)
+            m2(n - 6)
             e(n - 3)
-            g_(n - 4)
+            if not f_on_s(n - 4):
+                f(n - 4)
             c_(n - 1)

@@ -28,7 +28,7 @@ AHEAD = 3
 XBUFS = 5
 F_ON_S = (1,)
 F_MOD = 2
-D_ON_V = 30
+D_ON_V = 31
 E_ENG = "vector"
 SC_BUFS = 3
 WT_BUFS = 2
@@ -46,7 +46,7 @@ def tile_pattention_t_kernel(tc, inputs, key_param_tokens, value_param_tokens, o
         xin = ctx.enter_context(tc.tile_pool(name="xin", bufs=XBUFS))
         xgp = ctx.enter_context(tc.tile_pool(name="xgp", bufs=3))
         xqp = ctx.enter_context(tc.tile_pool(name="xqp", bufs=3))
-        gp = ctx.enter_context(tc.tile_pool(name="gp", bufs=8))
+        gp = ctx.enter_context(tc.tile_pool(name="gp", bufs=10))
         sp = ctx.enter_context(tc.tile_pool(name="sp", bufs=4))
         wp = ctx.enter_context(tc.tile_pool(name="wp", bufs=6))
         wgp = ctx.enter_context(tc.tile_pool(name="wgp", bufs=3))
@@ -315,22 +315,22 @@ def tile_pattention_t_kernel(tc, inputs, key_param_tokens, value_param_tokens, o
         m1(0)
         prep_v()
         c_(0)
-        for n in range(2, N_PAIRS + 8):
+        for n in range(2, N_PAIRS + 10):
             if n % 2 == 0:
                 load(n // 2 + AHEAD)
             b(n - 1)
-            g_(n - 5)
+            e(n - 4)
             tx(n)
-            tw(n - 4)
-            a(n)
+            tw(n - 5)
             d_(n - 2)
             p_(n - 2)
-            if f_on_s(n - 4):
-                f(n - 4)
-            h_(n - 7)
+            if f_on_s(n - 6):
+                f(n - 6)
+            h_(n - 9)
             m1(n - 1)
-            m2(n - 6)
-            e(n - 3)
-            if not f_on_s(n - 4):
-                f(n - 4)
+            m2(n - 8)
             c_(n - 1)
+            a(n)
+            if not f_on_s(n - 6):
+                f(n - 6)
+            g_(n - 7)

@@ -29,6 +29,7 @@ XBUFS = 5
 F_ON_S = (1,)
 F_MOD = 2
 D_ON_V = 31
+N_DUMMY = 3
 E_ENG = "vector"
 SC_BUFS = 3
 WT_BUFS = 2
@@ -51,7 +52,7 @@ def tile_pattention_t_kernel(tc, inputs, key_param_tokens, value_param_tokens, o
         wp = ctx.enter_context(tc.tile_pool(name="wp", bufs=6))
         wgp = ctx.enter_context(tc.tile_pool(name="wgp", bufs=3))
         wqp = ctx.enter_context(tc.tile_pool(name="wqp", bufs=3))
-        obp = ctx.enter_context(tc.tile_pool(name="obp", bufs=3))
+        obp = ctx.enter_context(tc.tile_pool(name="obp", bufs=4))
         psx = ctx.enter_context(tc.psum_pool(name="psx", bufs=2))
         pss = ctx.enter_context(tc.psum_pool(name="pss", bufs=SC_BUFS))
         psw = ctx.enter_context(tc.psum_pool(name="psw", bufs=WT_BUFS))
@@ -61,6 +62,8 @@ def tile_pattention_t_kernel(tc, inputs, key_param_tokens, value_param_tokens, o
 
         st = {}
 
+        wz = const.tile([P, 4 * P], BF16, name="wz")
+        nc.vector.memset(wz[:].bitcast(U32), 0)
         warm = const.tile([P, 1], F32, name="warm")
         nc.vector.memset(warm[:], 0.0)
         nc.scalar.activation(out=warm[:], in_=warm[:], func=ACT.Gelu)
@@ -82,11 +85,15 @@ def tile_pattention_t_kernel(tc, inputs, key_param_tokens, value_param_tokens, o
                 nc.sync.dma_start(out=x_sb[:, c : c + step], in_=xv[quad, :, c : c + step])
             st["x", quad] = x_sb
 
-        load(0, pieces=2)
+        load(0, pieces=4)
         v_sb = const.tile([P, 4 * DV], BF16, name="v_sb")
         nc.sync.dma_start(out=v_sb[:].rearrange("p (u c) -> p u c", u=2), in_=vv)
         for quad in range(1, AHEAD):
             load(quad)
+
+        dummy = pso.tile([P, 4, DV], F32, name="ot")
+        for i in range(N_DUMMY):
+            nc.tensor.matmul(out=dummy[:].rearrange("p j v -> p (j v)"), lhsT=wz[:, :P], rhs=wz[:], start=True, stop=True)
 
         kg = const.tile([P, 4 * D], BF16, name="kg", align_bytes=64)
         kgw = kg[:].bitcast(F32).rearrange("p (g t r u) -> p g t r u", g=2, t=4, r=P, u=2)
@@ -108,12 +115,14 @@ def tile_pattention_t_kernel(tc, inputs, key_param_tokens, value_param_tokens, o
             else:
                 nc.scalar.copy(out=kgw[:, :, t], in_=src)
 
-        def kb(g):
-            nc.vector.quantize_mx(
-                out=kq[:, g * S : (g + 1) * S].bitcast(FP8X4),
-                scales=ks[:, g * S : (g + 1) * S],
-                in_=kg[:, g * 4 * S : (g + 1) * 4 * S],
-            )
+        def kb(half):
+            for g in range(2):
+                c = g * S + half * S // 2
+                nc.vector.quantize_mx(
+                    out=kq[:, c : c + S // 2].bitcast(FP8X4),
+                    scales=ks[:, c : c + S // 2],
+                    in_=kg[:, 4 * c : 4 * c + 2 * S],
+                )
 
         vg = const.tile([P, 4 * DV], BF16, name="vg", align_bytes=64)
         vq = const.tile([P, DV], U32, name="vq", align_bytes=64)
@@ -243,6 +252,14 @@ def tile_pattention_t_kernel(tc, inputs, key_param_tokens, value_param_tokens, o
         def tw(q):
             if not ok(q):
                 return
+            if q == N_PAIRS - 1:
+                for h in range(2):
+                    ww = st["w", q, h][:].bitcast(F32)
+                    wl = psx.tile([P, 2, P], F32, name="xt")
+                    for u in range(2):
+                        nc.tensor.transpose(out=wl[:, u, :], in_=ww[:, u * P : (u + 1) * P], identity=idf[:])
+                    st["wl", h] = wl
+                return
             wt = psw.tile([P, 2, 2, P], F32, name="wt")
             for h in range(2):
                 ww = st["w", q, h][:].bitcast(F32)
@@ -257,6 +274,16 @@ def tile_pattention_t_kernel(tc, inputs, key_param_tokens, value_param_tokens, o
             if not ok(q):
                 return
             wg = wgp.tile([P, 2 * S], BF16, name="wg", align_bytes=64)
+            if q == N_PAIRS - 1:
+                for h in range(2):
+                    dst = wg[:, h * S : (h + 1) * S].bitcast(F32).rearrange("p (r u) -> p r u", r=P, u=2)
+                    src = st["wl", h][:].rearrange("p u r -> p r u")
+                    if h == 0:
+                        nc.vector.tensor_copy(out=dst, in_=src)
+                    else:
+                        nc.scalar.copy(out=dst, in_=src)
+                st["wg", q] = wg
+                return
             dst = wg[:].bitcast(F32).rearrange("p (h r u) -> p h r u", h=2, r=P, u=2)
             src = st["wt", q][:].rearrange("p h u r -> p h r u")
             if f_on_s(q):
@@ -270,18 +297,29 @@ def tile_pattention_t_kernel(tc, inputs, key_param_tokens, value_param_tokens, o
                 return
             wq = wqp.tile([P, 2 * P], U32, name="wq", align_bytes=64)
             ws = wqp.tile([P, 2 * P], U8, name="ws", align_bytes=64)
-            nc.vector.quantize_mx(out=wq[:].bitcast(FP8X4), scales=ws[:], in_=st["wg", q][:])
+            if q == N_PAIRS - 1:
+                for h in range(2):
+                    nc.vector.quantize_mx(out=wq[:, h * P : (h + 1) * P].bitcast(FP8X4), scales=ws[:, h * P : (h + 1) * P],
+                                          in_=st["wg", q][:, h * S : (h + 1) * S])
+            else:
+                nc.vector.quantize_mx(out=wq[:].bitcast(FP8X4), scales=ws[:], in_=st["wg", q][:])
             st["wq", q] = (wq, ws)
 
         def m2(q):
             if not ok(q):
                 return
-            if q % 2 == 0:
+            if q == N_PAIRS - 2:
+                ot = pss.tile([P, 4, DV], F32, name="sc")
+                st["ot", q // 2] = ot
+            elif q % 2 == 0:
                 ot = pso.tile([P, 4, DV], F32, name="ot")
                 st["ot", q // 2] = ot
-            ot = st["ot", q // 2]
             wq, ws = st["wq", q]
             for h in range(2):
+                ot = st["ot", q // 2]
+                if q == N_PAIRS - 1:
+                    ot = pss.tile([P, 4, DV], F32, name="sc")
+                    st["otl", h] = ot
                 nc.tensor.matmul_mx(
                     out=ot[:, 2 * (q % 2) + h, :],
                     lhsT=wq[:, h * P : (h + 1) * P].bitcast(FP8X4),
@@ -293,18 +331,29 @@ def tile_pattention_t_kernel(tc, inputs, key_param_tokens, value_param_tokens, o
                 )
 
         def h_(q):
-            if not ok(q) or q % 2 == 0:
+            if not ok(q) or (q % 2 == 0 and q < N_PAIRS - 2):
                 return
+            if q == N_PAIRS - 1:
+                for h in range(2):
+                    cols = slice((2 + h) * DV, (3 + h) * DV)
+                    ob = obp.tile([P, 4 * DV], F32, name="ob")
+                    if h == 0:
+                        nc.vector.tensor_copy(out=ob[:, cols], in_=st["otl", h][:, 2 + h, :])
+                    else:
+                        nc.scalar.copy(out=ob[:, cols], in_=st["otl", h][:, 2 + h, :])
+                    nc.sync.dma_start(out=ov[q // 2, :, cols], in_=ob[:, cols])
+                return
+            cols = slice(0, 4 * DV if q < N_PAIRS - 2 else 2 * DV)
             ob = obp.tile([P, 4 * DV], F32, name="ob")
-            nc.scalar.copy(out=ob[:], in_=st["ot", q // 2][:].rearrange("p j v -> p (j v)"))
-            nc.sync.dma_start(out=ov[q // 2], in_=ob[:])
+            nc.scalar.copy(out=ob[:, cols], in_=st["ot", q // 2][:].rearrange("p j v -> p (j v)")[:, cols])
+            nc.sync.dma_start(out=ov[q // 2, :, cols], in_=ob[:, cols])
 
         tx1(0, 0)
         tx1(0, 1)
         a1(0, 0, True)
         kb(0)
-        b(0, (0, 1))
         kb(1)
+        b(0, (0, 1))
         a1(0, 1, True)
         load(AHEAD)
         tx1(1, 0)

@@ -27,10 +27,10 @@ MANUAL = True
 AHEAD = 3
 XBUFS = 5
 F_ON_S = (1,)
-F_MOD = 2
+F_MOD = 3
+E_ON_G = range(0, 29)
 D_ON_V = 31
 N_DUMMY = 3
-E_ENG = "vector"
 SC_BUFS = 3
 WT_BUFS = 2
 
@@ -45,7 +45,7 @@ def tile_pattention_t_kernel(tc, inputs, key_param_tokens, value_param_tokens, o
     with ExitStack() as ctx:
         const = ctx.enter_context(tc.tile_pool(name="const", bufs=1))
         xin = ctx.enter_context(tc.tile_pool(name="xin", bufs=XBUFS))
-        xgp = ctx.enter_context(tc.tile_pool(name="xgp", bufs=3))
+        xgp = ctx.enter_context(tc.tile_pool(name="xgp", bufs=4))
         xqp = ctx.enter_context(tc.tile_pool(name="xqp", bufs=3))
         gp = ctx.enter_context(tc.tile_pool(name="gp", bufs=10))
         sp = ctx.enter_context(tc.tile_pool(name="sp", bufs=4))
@@ -240,21 +240,27 @@ def tile_pattention_t_kernel(tc, inputs, key_param_tokens, value_param_tokens, o
             if not ok(q):
                 return
             for h in range(2):
+                if h == 1 and q in E_ON_G:
+                    continue
                 w = wp.tile([P, S], BF16, name="w")
-                if E_ENG == "vector":
-                    nc.vector.tensor_scalar(out=w[:], in0=st["g", q, h][:], scalar1=st["r", q][:, h : h + 1],
-                                            scalar2=None, op0=ALU.mult)
-                else:
-                    nc.gpsimd.tensor_scalar(out=w[:], in0=st["g", q, h][:], scalar1=st["r", q][:, h : h + 1],
-                                            scalar2=0.0, op0=ALU.mult, op1=ALU.add)
-                st["w", q, h] = w
+                nc.vector.tensor_scalar(out=w[:], in0=st["g", q, h][:], scalar1=st["r", q][:, h : h + 1],
+                                        scalar2=None, op0=ALU.mult)
+                st["w", q, h] = w[:]
+
+        def eg(q):
+            if not ok(q) or q not in E_ON_G:
+                return
+            w = st["xg", q + 3][:, 0:S]
+            nc.gpsimd.tensor_scalar(out=w, in0=st["g", q, 1][:], scalar1=st["r", q][:, 1:2],
+                                    scalar2=1.0, op0=ALU.mult, op1=ALU.mult)
+            st["w", q, 1] = w
 
         def tw(q):
             if not ok(q):
                 return
             if q == N_PAIRS - 1:
                 for h in range(2):
-                    ww = st["w", q, h][:].bitcast(F32)
+                    ww = st["w", q, h].bitcast(F32)
                     wl = psx.tile([P, 2, P], F32, name="xt")
                     for u in range(2):
                         nc.tensor.transpose(out=wl[:, u, :], in_=ww[:, u * P : (u + 1) * P], identity=idf[:])
@@ -262,7 +268,7 @@ def tile_pattention_t_kernel(tc, inputs, key_param_tokens, value_param_tokens, o
                 return
             wt = psw.tile([P, 2, 2, P], F32, name="wt")
             for h in range(2):
-                ww = st["w", q, h][:].bitcast(F32)
+                ww = st["w", q, h].bitcast(F32)
                 for u in range(2):
                     nc.tensor.transpose(out=wt[:, h, u, :], in_=ww[:, u * P : (u + 1) * P], identity=idf[:])
             st["wt", q] = wt
@@ -367,8 +373,10 @@ def tile_pattention_t_kernel(tc, inputs, key_param_tokens, value_param_tokens, o
         for n in range(2, N_PAIRS + 10):
             if n % 2 == 0:
                 load(n // 2 + AHEAD)
-            b(n - 1)
             e(n - 4)
+            g_(n - 8)
+            b(n - 1)
+            eg(n - 4)
             tx(n)
             tw(n - 5)
             d_(n - 2)
@@ -382,4 +390,3 @@ def tile_pattention_t_kernel(tc, inputs, key_param_tokens, value_param_tokens, o
             a(n)
             if not f_on_s(n - 6):
                 f(n - 6)
-            g_(n - 7)

@@ -27,9 +27,9 @@ MANUAL = True
 AHEAD = 3
 XBUFS = 5
 F_ON_S = (1,)
-F_MOD = 3
+F_MOD = 4
 E_ON_G = range(0, 29)
-D_ON_V = 31
+LAST = N_PAIRS - 1
 N_DUMMY = 3
 SC_BUFS = 3
 WT_BUFS = 2
@@ -50,9 +50,9 @@ def tile_pattention_t_kernel(tc, inputs, key_param_tokens, value_param_tokens, o
         gp = ctx.enter_context(tc.tile_pool(name="gp", bufs=10))
         sp = ctx.enter_context(tc.tile_pool(name="sp", bufs=4))
         wp = ctx.enter_context(tc.tile_pool(name="wp", bufs=6))
-        wgp = ctx.enter_context(tc.tile_pool(name="wgp", bufs=3))
+        wgp = ctx.enter_context(tc.tile_pool(name="wgp", bufs=5))
         wqp = ctx.enter_context(tc.tile_pool(name="wqp", bufs=3))
-        obp = ctx.enter_context(tc.tile_pool(name="obp", bufs=4))
+        obp = ctx.enter_context(tc.tile_pool(name="obp", bufs=7))
         psx = ctx.enter_context(tc.psum_pool(name="psx", bufs=2))
         pss = ctx.enter_context(tc.psum_pool(name="pss", bufs=SC_BUFS))
         psw = ctx.enter_context(tc.psum_pool(name="psw", bufs=WT_BUFS))
@@ -215,18 +215,11 @@ def tile_pattention_t_kernel(tc, inputs, key_param_tokens, value_param_tokens, o
             ss = sp.tile([P, 2], F32, name="ss")
             for h in range(2):
                 g = st["g", q, h]
-                if h == 1 and q >= D_ON_V:
-                    junk = sp.tile([P, S], BF16, name="junkv")
-                    nc.vector.scalar_tensor_tensor(
-                        out=junk[:], in0=g[:], scalar=1.0 / S, in1=g[:],
-                        op0=ALU.mult, op1=ALU.mult, accum_out=ss[:, h : h + 1],
-                    )
-                else:
-                    junk = sp.tile([P, S], BF16, name="junk")
-                    nc.scalar.activation(
-                        out=junk[:], in_=g[:], func=ACT.Square,
-                        scale=1.0 / math.sqrt(float(S)), accum_out=ss[:, h : h + 1],
-                    )
+                junk = sp.tile([P, S], BF16, name="junk")
+                nc.scalar.activation(
+                    out=junk[:], in_=g[:], func=ACT.Square,
+                    scale=1.0 / math.sqrt(float(S)), accum_out=ss[:, h : h + 1],
+                )
             st["ss", q] = ss
 
         def p_(q):
@@ -258,14 +251,6 @@ def tile_pattention_t_kernel(tc, inputs, key_param_tokens, value_param_tokens, o
         def tw(q):
             if not ok(q):
                 return
-            if q == N_PAIRS - 1:
-                for h in range(2):
-                    ww = st["w", q, h].bitcast(F32)
-                    wl = psx.tile([P, 2, P], F32, name="xt")
-                    for u in range(2):
-                        nc.tensor.transpose(out=wl[:, u, :], in_=ww[:, u * P : (u + 1) * P], identity=idf[:])
-                    st["wl", h] = wl
-                return
             wt = psw.tile([P, 2, 2, P], F32, name="wt")
             for h in range(2):
                 ww = st["w", q, h].bitcast(F32)
@@ -276,23 +261,15 @@ def tile_pattention_t_kernel(tc, inputs, key_param_tokens, value_param_tokens, o
         def f_on_s(q):
             return q % F_MOD in F_ON_S
 
-        def f(q):
+        def f(q, on_scalar=None):
             if not ok(q):
                 return
+            if on_scalar is None:
+                on_scalar = f_on_s(q)
             wg = wgp.tile([P, 2 * S], BF16, name="wg", align_bytes=64)
-            if q == N_PAIRS - 1:
-                for h in range(2):
-                    dst = wg[:, h * S : (h + 1) * S].bitcast(F32).rearrange("p (r u) -> p r u", r=P, u=2)
-                    src = st["wl", h][:].rearrange("p u r -> p r u")
-                    if h == 0:
-                        nc.vector.tensor_copy(out=dst, in_=src)
-                    else:
-                        nc.scalar.copy(out=dst, in_=src)
-                st["wg", q] = wg
-                return
             dst = wg[:].bitcast(F32).rearrange("p (h r u) -> p h r u", h=2, r=P, u=2)
             src = st["wt", q][:].rearrange("p h u r -> p h r u")
-            if f_on_s(q):
+            if on_scalar:
                 nc.scalar.copy(out=dst, in_=src)
             else:
                 nc.vector.tensor_copy(out=dst, in_=src)
@@ -303,56 +280,97 @@ def tile_pattention_t_kernel(tc, inputs, key_param_tokens, value_param_tokens, o
                 return
             wq = wqp.tile([P, 2 * P], U32, name="wq", align_bytes=64)
             ws = wqp.tile([P, 2 * P], U8, name="ws", align_bytes=64)
-            if q == N_PAIRS - 1:
-                for h in range(2):
-                    nc.vector.quantize_mx(out=wq[:, h * P : (h + 1) * P].bitcast(FP8X4), scales=ws[:, h * P : (h + 1) * P],
-                                          in_=st["wg", q][:, h * S : (h + 1) * S])
-            else:
-                nc.vector.quantize_mx(out=wq[:].bitcast(FP8X4), scales=ws[:], in_=st["wg", q][:])
+            nc.vector.quantize_mx(out=wq[:].bitcast(FP8X4), scales=ws[:], in_=st["wg", q][:])
             st["wq", q] = (wq, ws)
+
+        def m2_1(q, h, ot, slot):
+            wq, ws = st["wq", q]
+            nc.tensor.matmul_mx(
+                out=ot[:, slot, :],
+                lhsT=wq[:, h * P : (h + 1) * P].bitcast(FP8X4),
+                lhsT_scale=ws[:, h * P : (h + 1) * P],
+                rhs=vq[:].bitcast(FP8X4),
+                rhs_scale=vs[:],
+                start=True,
+                stop=True,
+            )
 
         def m2(q):
             if not ok(q):
                 return
-            if q == N_PAIRS - 2:
-                ot = pss.tile([P, 4, DV], F32, name="sc")
-                st["ot", q // 2] = ot
-            elif q % 2 == 0:
-                ot = pso.tile([P, 4, DV], F32, name="ot")
-                st["ot", q // 2] = ot
-            wq, ws = st["wq", q]
-            for h in range(2):
-                ot = st["ot", q // 2]
-                if q == N_PAIRS - 1:
+            if q % 2 == 0:
+                if q < N_PAIRS - 6:
+                    ot = pso.tile([P, 4, DV], F32, name="ot")
+                else:
                     ot = pss.tile([P, 4, DV], F32, name="sc")
-                    st["otl", h] = ot
-                nc.tensor.matmul_mx(
-                    out=ot[:, 2 * (q % 2) + h, :],
-                    lhsT=wq[:, h * P : (h + 1) * P].bitcast(FP8X4),
-                    lhsT_scale=ws[:, h * P : (h + 1) * P],
-                    rhs=vq[:].bitcast(FP8X4),
-                    rhs_scale=vs[:],
-                    start=True,
-                    stop=True,
-                )
+                st["ot", q // 2] = ot
+            for h in range(2):
+                m2_1(q, h, st["ot", q // 2], 2 * (q % 2) + h)
+
+        def store(quad, ot, lo, hi, on_scalar=True):
+            cols = slice(lo * DV, hi * DV)
+            ob = obp.tile([P, 4 * DV], F32, name="ob")
+            src = ot[:].rearrange("p j v -> p (j v)")[:, cols]
+            if on_scalar:
+                nc.scalar.copy(out=ob[:, cols], in_=src)
+            else:
+                nc.vector.tensor_copy(out=ob[:, cols], in_=src)
+            nc.sync.dma_start(out=ov[quad, :, cols], in_=ob[:, cols])
 
         def h_(q):
-            if not ok(q) or (q % 2 == 0 and q < N_PAIRS - 2):
-                return
-            if q == N_PAIRS - 1:
-                for h in range(2):
-                    cols = slice((2 + h) * DV, (3 + h) * DV)
-                    ob = obp.tile([P, 4 * DV], F32, name="ob")
-                    if h == 0:
-                        nc.vector.tensor_copy(out=ob[:, cols], in_=st["otl", h][:, 2 + h, :])
-                    else:
-                        nc.scalar.copy(out=ob[:, cols], in_=st["otl", h][:, 2 + h, :])
-                    nc.sync.dma_start(out=ov[q // 2, :, cols], in_=ob[:, cols])
-                return
-            cols = slice(0, 4 * DV if q < N_PAIRS - 2 else 2 * DV)
-            ob = obp.tile([P, 4 * DV], F32, name="ob")
-            nc.scalar.copy(out=ob[:, cols], in_=st["ot", q // 2][:].rearrange("p j v -> p (j v)")[:, cols])
-            nc.sync.dma_start(out=ov[q // 2, :, cols], in_=ob[:, cols])
+            if ok(q) and q % 2 == 1:
+                store(q // 2, st["ot", q // 2], 0, 4)
+
+        def last_dp(h, on_scalar):
+            g = st["g", LAST, h]
+            ss = sp.tile([P, 2], F32, name="ss")
+            if on_scalar:
+                junk = sp.tile([P, S], BF16, name="junk")
+                nc.scalar.activation(
+                    out=junk[:], in_=g[:], func=ACT.Square,
+                    scale=1.0 / math.sqrt(float(S)), accum_out=ss[:, 0:1],
+                )
+            else:
+                junk = sp.tile([P, S], BF16, name="junkv")
+                nc.vector.scalar_tensor_tensor(
+                    out=junk[:], in0=g[:], scalar=1.0 / S, in1=g[:],
+                    op0=ALU.mult, op1=ALU.mult, accum_out=ss[:, 0:1],
+                )
+            r = sp.tile([P, 2], F32, name="r")
+            nc.gpsimd.tensor_tensor(out=r[:, 0:1], in0=ss[:, 0:1], in1=neg_half[:, 0:1], op=ALU.pow)
+            st["rl", h] = r
+
+        def last_e(h):
+            w = wp.tile([P, S], BF16, name="w")
+            nc.vector.tensor_scalar(out=w[:], in0=st["g", LAST, h][:], scalar1=st["rl", h][:, 0:1],
+                                    scalar2=None, op0=ALU.mult)
+            ww = w[:].bitcast(F32)
+            wl = psx.tile([P, 2, P], F32, name="xt")
+            for u in range(2):
+                nc.tensor.transpose(out=wl[:, u, :], in_=ww[:, u * P : (u + 1) * P], identity=idf[:])
+            st["wl", h] = wl
+
+        def last_f(h, on_scalar):
+            wg = wgp.tile([P, 2 * S], BF16, name="wg", align_bytes=64)
+            dst = wg[:, 0:S].bitcast(F32).rearrange("p (r u) -> p r u", r=P, u=2)
+            src = st["wl", h][:].rearrange("p u r -> p r u")
+            if on_scalar:
+                nc.scalar.copy(out=dst, in_=src)
+            else:
+                nc.vector.tensor_copy(out=dst, in_=src)
+            st["wgl", h] = wg
+
+        def last_gm(h):
+            wq = wqp.tile([P, 2 * P], U32, name="wq", align_bytes=64)
+            ws = wqp.tile([P, 2 * P], U8, name="ws", align_bytes=64)
+            nc.vector.quantize_mx(out=wq[:, 0:P].bitcast(FP8X4), scales=ws[:, 0:P], in_=st["wgl", h][:, 0:S])
+            st["wq", "l%d" % h] = (wq, ws)
+            if h == 0:
+                ot = pso.tile([P, 4, DV], F32, name="ot")
+            else:
+                ot = pss.tile([P, 4, DV], F32, name="sc")
+            st["otl", h] = ot
+            m2_1("l%d" % h, 0, ot, 2 + h)
 
         tx1(0, 0)
         tx1(0, 1)
@@ -370,7 +388,7 @@ def tile_pattention_t_kernel(tc, inputs, key_param_tokens, value_param_tokens, o
         m1(0)
         prep_v()
         c_(0)
-        for n in range(2, N_PAIRS + 10):
+        for n in range(2, N_PAIRS + 1):
             if n % 2 == 0:
                 load(n // 2 + AHEAD)
             e(n - 4)
@@ -390,3 +408,38 @@ def tile_pattention_t_kernel(tc, inputs, key_param_tokens, value_param_tokens, o
             a(n)
             if not f_on_s(n - 6):
                 f(n - 6)
+        e(LAST - 2)
+        tw(LAST - 3)
+        f(LAST - 4, on_scalar=False)
+        g_(LAST - 6)
+        m2(LAST - 6)
+        e(LAST - 1)
+        tw(LAST - 2)
+        last_dp(0, on_scalar=False)
+        last_dp(1, on_scalar=True)
+        f(LAST - 3, on_scalar=True)
+        h_(LAST - 6)
+        g_(LAST - 5)
+        m2(LAST - 5)
+        f(LAST - 2, on_scalar=False)
+        tw(LAST - 1)
+        last_e(0)
+        g_(LAST - 4)
+        m2(LAST - 4)
+        last_e(1)
+        f(LAST - 1, on_scalar=True)
+        g_(LAST - 3)
+        m2(LAST - 3)
+        last_f(0, on_scalar=False)
+        last_f(1, on_scalar=True)
+        h_(LAST - 4)
+        g_(LAST - 2)
+        m2(LAST - 2)
+        last_gm(0)
+        g_(LAST - 1)
+        m2(LAST - 1)
+        last_gm(1)
+        h_(LAST - 2)
+        store(LAST // 2, st["ot", LAST // 2], 0, 2, on_scalar=False)
+        store(LAST // 2, st["otl", 0], 2, 3, on_scalar=False)
+        store(LAST // 2, st["otl", 1], 3, 4)

from contextlib import ExitStack
import math

import concourse.bass as bass
import concourse.mybir as mybir
import concourse.tile as tile
from concourse.masks import make_identity

F32 = mybir.dt.float32
BF16 = mybir.dt.bfloat16
U32 = mybir.dt.uint32
U8 = mybir.dt.uint8
FP8X4 = mybir.dt.float8_e4m3fn_x4
ACT = mybir.ActivationFunctionType
ALU = mybir.AluOpType

P = 128
TOKENS = 8192
D = 1024
S = 512
DV = 128
N_QUADS = TOKENS // (4 * P)
N_PAIRS = 2 * N_QUADS
FLOPS = 2 * TOKENS * D * S + 2 * TOKENS * S * DV

MANUAL = True
AHEAD = 3
XBUFS = 5
F_ON_S = (1,)
F_MOD = 4
E_ON_G = range(0, 29)
LAST = N_PAIRS - 1
N_DUMMY = 3
SC_BUFS = 3
WT_BUFS = 2


def tile_pattention_t_kernel(tc, inputs, key_param_tokens, value_param_tokens, out):
    nc = tc.nc
    xv = inputs.flatten_outer_dims().rearrange("(n p j) d -> n p (j d)", p=P, j=4)
    ov = out.flatten_outer_dims().rearrange("(n p j) v -> n p (j v)", p=P, j=4)
    kv = key_param_tokens.rearrange("(t p) d -> t p d", p=P)
    vv = value_param_tokens.rearrange("(u p e) v -> p u (e v)", u=2, e=2)

    with ExitStack() as ctx:
        const = ctx.enter_context(tc.tile_pool(name="const", bufs=1))
        xin = ctx.enter_context(tc.tile_pool(name="xin", bufs=XBUFS))
        xgp = ctx.enter_context(tc.tile_pool(name="xgp", bufs=4))
        xqp = ctx.enter_context(tc.tile_pool(name="xqp", bufs=3))
        gp = ctx.enter_context(tc.tile_pool(name="gp", bufs=10))
        sp = ctx.enter_context(tc.tile_pool(name="sp", bufs=4))
        wp = ctx.enter_context(tc.tile_pool(name="wp", bufs=6))
        wgp = ctx.enter_context(tc.tile_pool(name="wgp", bufs=5))
        wqp = ctx.enter_context(tc.tile_pool(name="wqp", bufs=3))
        obp = ctx.enter_context(tc.tile_pool(name="obp", bufs=7))
        psx = ctx.enter_context(tc.psum_pool(name="psx", bufs=2))
        pss = ctx.enter_context(tc.psum_pool(name="pss", bufs=SC_BUFS))
        psw = ctx.enter_context(tc.psum_pool(name="psw", bufs=WT_BUFS))
        pso = ctx.enter_context(tc.psum_pool(name="pso", bufs=1))
        if MANUAL:
            ctx.enter_context(tc.manual_schedule())

        st = {}

        wz = const.tile([P, 4 * P], BF16, name="wz")
        nc.vector.memset(wz[:].bitcast(U32), 0)
        warm = const.tile([P, 1], F32, name="warm")
        nc.vector.memset(warm[:], 0.0)
        nc.scalar.activation(out=warm[:], in_=warm[:], func=ACT.Gelu)
        neg_half = const.tile([P, 2], F32, name="neg_half")
        nc.vector.memset(neg_half[:], -0.5)
        idf = const.tile([P, P], F32, name="idf")
        make_identity(nc, idf[:])

        k_sb = const.tile([P, 4 * D], BF16, name="k_sb")
        for t in range(4):
            nc.sync.dma_start(out=k_sb[:, t * D : (t + 1) * D], in_=kv[t])

        def load(quad, pieces=1):
            if quad >= N_QUADS:
                return
            x_sb = xin.tile([P, 4 * D], BF16, name="x_sb")
            step = 4 * D // pieces
            for c in range(0, 4 * D, step):
                nc.sync.dma_start(out=x_sb[:, c : c + step], in_=xv[quad, :, c : c + step])
            st["x", quad] = x_sb

        load(0, pieces=4)
        v_sb = const.tile([P, 4 * DV], BF16, name="v_sb")
        nc.sync.dma_start(out=v_sb[:].rearrange("p (u c) -> p u c", u=2), in_=vv)
        for quad in range(1, AHEAD):
            load(quad)

        dummy = pso.tile([P, 4, DV], F32, name="ot")
        for i in range(N_DUMMY):
            nc.tensor.matmul(out=dummy[:].rearrange("p j v -> p (j v)"), lhsT=wz[:, :P], rhs=wz[:], start=True, stop=True)

        kg = const.tile([P, 4 * D], BF16, name="kg", align_bytes=64)
        kgw = kg[:].bitcast(F32).rearrange("p (g t r u) -> p g t r u", g=2, t=4, r=P, u=2)
        kq = const.tile([P, 2 * S], U32, name="kq", align_bytes=64)
        ks = const.tile([P, 2 * S], U8, name="ks", align_bytes=64)
        kw = k_sb[:].bitcast(F32)
        for t in range(4):
            if t < 2:
                kt = psx.tile([P, 2, 2, P], F32, name="xt")
            else:
                kt = pss.tile([P, 2, 2, P], F32, name="sc")
            for g in range(2):
                for u in range(2):
                    c = (4 * t + 2 * g + u) * P
                    nc.tensor.transpose(out=kt[:, g, u, :], in_=kw[:, c : c + P], identity=idf[:])
            src = kt[:].rearrange("p g u r -> p g r u")
            if t % 2 == 0:
                nc.vector.tensor_copy(out=kgw[:, :, t], in_=src)
            else:
                nc.scalar.copy(out=kgw[:, :, t], in_=src)

        def kb(half):
            for g in range(2):
                c = g * S + half * S // 2
                nc.vector.quantize_mx(
                    out=kq[:, c : c + S // 2].bitcast(FP8X4),
                    scales=ks[:, c : c + S // 2],
                    in_=kg[:, 4 * c : 4 * c + 2 * S],
                )

        vg = const.tile([P, 4 * DV], BF16, name="vg", align_bytes=64)
        vq = const.tile([P, DV], U32, name="vq", align_bytes=64)
        vs = const.tile([P, DV], U8, name="vs", align_bytes=64)

        def prep_v():
            nc.vector.tensor_copy(
                out=vg[:].rearrange("p (v j) -> p v j", j=4),
                in_=v_sb[:].rearrange("p (j v) -> p v j", j=4),
            )
            nc.vector.quantize_mx(out=vq[:].bitcast(FP8X4), scales=vs[:], in_=vg[:])

        def ok(q):
            return 0 <= q < N_PAIRS

        def tx1(q, h):
            xw = st["x", q // 2][:].bitcast(F32)
            j = 2 * (q % 2) + h
            xt = psx.tile([P, 2, 2, P], F32, name="xt")
            for g in range(2):
                for u in range(2):
                    c = (4 * j + 2 * g + u) * P
                    nc.tensor.transpose(out=xt[:, g, u, :], in_=xw[:, c : c + P], identity=idf[:])
            st["xt", q, h] = xt

        def tx(q):
            if ok(q):
                tx1(q, 0)
                tx1(q, 1)

        def a1(q, h, on_scalar=False):
            if h == 0:
                xg = xgp.tile([P, 2 * D], BF16, name="xg", align_bytes=64)
                st["xg", q] = xg
            xgw = st["xg", q][:].bitcast(F32).rearrange("p (h g r u) -> p h g r u", h=2, g=2, r=P, u=2)
            src = st["xt", q, h][:].rearrange("p g u r -> p g r u")
            if on_scalar:
                nc.scalar.copy(out=xgw[:, h], in_=src)
            else:
                nc.vector.tensor_copy(out=xgw[:, h], in_=src)

        def a(q):
            if ok(q):
                a1(q, 0)
                a1(q, 1)

        def b(q, halves=(0, 2)):
            if not ok(q):
                return
            h0, h1 = halves
            if h0 == 0:
                xq = xqp.tile([P, D // 2], U32, name="xq", align_bytes=64)
                xs = xqp.tile([P, D // 2], U8, name="xs", align_bytes=64)
                st["xq", q] = (xq, xs)
            xq, xs = st["xq", q]
            cols = slice(h0 * D // 4, h1 * D // 4)
            nc.vector.quantize_mx(out=xq[:, cols].bitcast(FP8X4), scales=xs[:, cols],
                                  in_=st["xg", q][:, h0 * D : h1 * D])

        def m1(q):
            if not ok(q):
                return
            xq, xs = st["xq", q]
            for h in range(2):
                sc = pss.tile([P, S], F32, name="sc")
                for g in range(2):
                    c = (2 * h + g) * P
                    nc.tensor.matmul_mx(
                        out=sc[:],
                        lhsT=xq[:, c : c + P].bitcast(FP8X4),
                        lhsT_scale=xs[:, c : c + P],
                        rhs=kq[:, g * S : (g + 1) * S].bitcast(FP8X4),
                        rhs_scale=ks[:, g * S : (g + 1) * S],
                        start=(g == 0),
                        stop=(g == 1),
                    )
                st["sc", q, h] = sc

        def c_(q):
            if not ok(q):
                return
            for h in range(2):
                gt = gp.tile([P, S], F32, name="gt")
                nc.scalar.activation(out=gt[:], in_=st["sc", q, h][:], func=ACT.Gelu)
                st["g", q, h] = gt

        def d_(q):
            if not ok(q):
                return
            ss = sp.tile([P, 2], F32, name="ss")
            for h in range(2):
                g = st["g", q, h]
                junk = sp.tile([P, S], BF16, name="junk")
                nc.scalar.activation(
                    out=junk[:], in_=g[:], func=ACT.Square,
                    scale=1.0 / math.sqrt(float(S)), accum_out=ss[:, h : h + 1],
                )
            st["ss", q] = ss

        def p_(q):
            if not ok(q):
                return
            r = sp.tile([P, 2], F32, name="r")
            nc.gpsimd.tensor_tensor(out=r[:], in0=st["ss", q][:], in1=neg_half[:], op=ALU.pow)
            st["r", q] = r

        def e(q):
            if not ok(q):
                return
            for h in range(2):
                if h == 1 and q in E_ON_G:
                    continue
                w = wp.tile([P, S], BF16, name="w")
                nc.vector.tensor_scalar(out=w[:], in0=st["g", q, h][:], scalar1=st["r", q][:, h : h + 1],
                                        scalar2=None, op0=ALU.mult)
                st["w", q, h] = w[:]

        def eg(q):
            if not ok(q) or q not in E_ON_G:
                return
            w = st["xg", q + 3][:, 0:S]
            nc.gpsimd.tensor_scalar(out=w, in0=st["g", q, 1][:], scalar1=st["r", q][:, 1:2],
                                    scalar2=1.0, op0=ALU.mult, op1=ALU.mult)
            st["w", q, 1] = w

        def tw(q):
            if not ok(q):
                return
            wt = psw.tile([P, 2, 2, P], F32, name="wt")
            for h in range(2):
                ww = st["w", q, h].bitcast(F32)
                for u in range(2):
                    nc.tensor.transpose(out=wt[:, h, u, :], in_=ww[:, u * P : (u + 1) * P], identity=idf[:])
            st["wt", q] = wt

        def f_on_s(q):
            return q % F_MOD in F_ON_S

        def f(q, on_scalar=None):
            if not ok(q):
                return
            if on_scalar is None:
                on_scalar = f_on_s(q)
            wg = wgp.tile([P, 2 * S], BF16, name="wg", align_bytes=64)
            dst = wg[:].bitcast(F32).rearrange("p (h r u) -> p h r u", h=2, r=P, u=2)
            src = st["wt", q][:].rearrange("p h u r -> p h r u")
            if on_scalar:
                nc.scalar.copy(out=dst, in_=src)
            else:
                nc.vector.tensor_copy(out=dst, in_=src)
            st["wg", q] = wg

        def g_(q):
            if not ok(q):
                return
            wq = wqp.tile([P, 2 * P], U32, name="wq", align_bytes=64)
            ws = wqp.tile([P, 2 * P], U8, name="ws", align_bytes=64)
            nc.vector.quantize_mx(out=wq[:].bitcast(FP8X4), scales=ws[:], in_=st["wg", q][:])
            st["wq", q] = (wq, ws)

        def m2_1(q, h, ot, slot):
            wq, ws = st["wq", q]
            nc.tensor.matmul_mx(
                out=ot[:, slot, :],
                lhsT=wq[:, h * P : (h + 1) * P].bitcast(FP8X4),
                lhsT_scale=ws[:, h * P : (h + 1) * P],
                rhs=vq[:].bitcast(FP8X4),
                rhs_scale=vs[:],
                start=True,
                stop=True,
            )

        def m2(q):
            if not ok(q):
                return
            if q % 2 == 0:
                if q < N_PAIRS - 6:
                    ot = pso.tile([P, 4, DV], F32, name="ot")
                else:
                    ot = pss.tile([P, 4, DV], F32, name="sc")
                st["ot", q // 2] = ot
            for h in range(2):
                m2_1(q, h, st["ot", q // 2], 2 * (q % 2) + h)

        def store(quad, ot, lo, hi, on_scalar=True):
            cols = slice(lo * DV, hi * DV)
            ob = obp.tile([P, 4 * DV], F32, name="ob")
            src = ot[:].rearrange("p j v -> p (j v)")[:, cols]
            if on_scalar:
                nc.scalar.copy(out=ob[:, cols], in_=src)
            else:
                nc.vector.tensor_copy(out=ob[:, cols], in_=src)
            nc.sync.dma_start(out=ov[quad, :, cols], in_=ob[:, cols])

        def h_(q):
            if ok(q) and q % 2 == 1:
                store(q // 2, st["ot", q // 2], 0, 4)

        def last_dp(h, on_scalar):
            g = st["g", LAST, h]
            ss = sp.tile([P, 2], F32, name="ss")
            if on_scalar:
                junk = sp.tile([P, S], BF16, name="junk")
                nc.scalar.activation(
                    out=junk[:], in_=g[:], func=ACT.Square,
                    scale=1.0 / math.sqrt(float(S)), accum_out=ss[:, 0:1],
                )
            else:
                junk = sp.tile([P, S], BF16, name="junkv")
                nc.vector.scalar_tensor_tensor(
                    out=junk[:], in0=g[:], scalar=1.0 / S, in1=g[:],
                    op0=ALU.mult, op1=ALU.mult, accum_out=ss[:, 0:1],
                )
            r = sp.tile([P, 2], F32, name="r")
            nc.gpsimd.tensor_tensor(out=r[:, 0:1], in0=ss[:, 0:1], in1=neg_half[:, 0:1], op=ALU.pow)
            st["rl", h] = r

        def last_e(h):
            w = wp.tile([P, S], BF16, name="w")
            nc.vector.tensor_scalar(out=w[:], in0=st["g", LAST, h][:], scalar1=st["rl", h][:, 0:1],
                                    scalar2=None, op0=ALU.mult)
            ww = w[:].bitcast(F32)
            wl = psx.tile([P, 2, P], F32, name="xt")
            for u in range(2):
                nc.tensor.transpose(out=wl[:, u, :], in_=ww[:, u * P : (u + 1) * P], identity=idf[:])
            st["wl", h] = wl

        def last_f(h, on_scalar):
            wg = wgp.tile([P, 2 * S], BF16, name="wg", align_bytes=64)
            dst = wg[:, 0:S].bitcast(F32).rearrange("p (r u) -> p r u", r=P, u=2)
            src = st["wl", h][:].rearrange("p u r -> p r u")
            if on_scalar:
                nc.scalar.copy(out=dst, in_=src)
            else:
                nc.vector.tensor_copy(out=dst, in_=src)
            st["wgl", h] = wg

        def last_gm(h):
            wq = wqp.tile([P, 2 * P], U32, name="wq", align_bytes=64)
            ws = wqp.tile([P, 2 * P], U8, name="ws", align_bytes=64)
            nc.vector.quantize_mx(out=wq[:, 0:P].bitcast(FP8X4), scales=ws[:, 0:P], in_=st["wgl", h][:, 0:S])
            st["wq", "l%d" % h] = (wq, ws)
            if h == 0:
                ot = pso.tile([P, 4, DV], F32, name="ot")
            else:
                ot = pss.tile([P, 4, DV], F32, name="sc")
            st["otl", h] = ot
            m2_1("l%d" % h, 0, ot, 2 + h)

        tx1(0, 0)
        tx1(0, 1)
        a1(0, 0, True)
        kb(0)
        kb(1)
        b(0, (0, 1))
        a1(0, 1, True)
        load(AHEAD)
        tx1(1, 0)
        a1(1, 0, True)
        tx1(1, 1)
        b(0, (1, 2))
        a1(1, 1)
        m1(0)
        prep_v()
        c_(0)
        for n in range(2, N_PAIRS + 1):
            if n % 2 == 0:
                load(n // 2 + AHEAD)
            e(n - 4)
            g_(n - 8)
            b(n - 1)
            eg(n - 4)
            tx(n)
            tw(n - 5)
            d_(n - 2)
            p_(n - 2)
            if f_on_s(n - 6):
                f(n - 6)
            h_(n - 9)
            m1(n - 1)
            m2(n - 8)
            c_(n - 1)
            a(n)
            if not f_on_s(n - 6):
                f(n - 6)
        e(LAST - 2)
        tw(LAST - 3)
        f(LAST - 4, on_scalar=False)
        g_(LAST - 6)
        m2(LAST - 6)
        e(LAST - 1)
        tw(LAST - 2)
        last_dp(0, on_scalar=False)
        last_dp(1, on_scalar=True)
        f(LAST - 3, on_scalar=True)
        h_(LAST - 6)
        g_(LAST - 5)
        m2(LAST - 5)
        f(LAST - 2, on_scalar=False)
        tw(LAST - 1)
        last_e(0)
        g_(LAST - 4)
        m2(LAST - 4)
        last_e(1)
        f(LAST - 1, on_scalar=True)
        g_(LAST - 3)
        m2(LAST - 3)
        last_f(0, on_scalar=False)
        last_f(1, on_scalar=True)
        h_(LAST - 4)
        g_(LAST - 2)
        m2(LAST - 2)
        last_gm(0)
        g_(LAST - 1)
        m2(LAST - 1)
        last_gm(1)
        h_(LAST - 2)
        store(LAST // 2, st["ot", LAST // 2], 0, 2, on_scalar=False)
        store(LAST // 2, st["otl", 0], 2, 3, on_scalar=False)
        store(LAST // 2, st["otl", 1], 3, 4)
